import numpy as np
import ml_dtypes


def mxq(x, axis, fmt="e4m3"):
    dtype, down = {"e4m3": (ml_dtypes.float8_e4m3fn, 7), "e5m2": (ml_dtypes.float8_e5m2, 14)}[fmt]
    v = np.moveaxis(np.asarray(x, np.float32).astype(ml_dtypes.bfloat16).astype(np.float64), axis, -1)
    blocks = v.reshape(v.shape[:-1] + (-1, 32))
    amax = np.abs(blocks).max(-1, keepdims=True)
    byte = np.maximum(np.where(amax > 0, np.frexp(amax)[1] - 1 + 127, 0) - down, 1)
    scale = np.exp2(byte - 127.0)
    codes = (blocks / scale).astype(np.float32).astype(dtype).astype(np.float64)
    return np.moveaxis((codes * scale).reshape(v.shape), -1, axis)


WIDE = False


def mx_kscale(k):
    if not WIDE:
        return np.ones(k)
    levels = np.array([10, -10, 5, -5, 0])
    if k % 512:
        return np.exp2(np.random.permutation(np.resize(levels, k // 32))).repeat(32)
    a = np.empty((k // 512, 16))
    for p in range(k // 512):
        a[p, :8] = np.random.permutation(np.resize(levels, 8))
        for g in range(8):
            far = levels[np.abs(levels - a[p, g]) >= 10]
            a[p, g + 8] = far[np.random.randint(len(far))]
    return np.exp2(a.ravel()).repeat(32)


BF16 = ml_dtypes.bfloat16


def bf(x):
    return np.asarray(x, np.float32).astype(BF16)


def f64(x):
    return np.asarray(x).astype(np.float64)


B, N, T, D, DO, H, E = 128, 2, 8, 512, 512, 8, 128
S = N * T


def sigmoid(v):
    return 1.0 / (1.0 + np.exp(-v))


def setup_inputs():
    r = np.random.standard_normal
    s = mx_kscale(B * S).reshape(B, S, 1)
    u = mx_kscale(DO)
    x0 = bf(r((B, S, D)))
    e = bf(r((B, E)))
    Wv0 = bf(r((D, DO)) / np.sqrt(D))
    bv = bf(r(DO) * 0.3)
    Wgate = bf(r((E, DO)) / np.sqrt(E))
    bgate = bf(r(DO) * 0.3)
    Wscale = bf(r((E, DO)) * 0.7 / np.sqrt(E))
    bscale = bf(r(DO) * 0.3)
    Wshift = bf(r((E, DO)) * 0.7 / np.sqrt(E))
    bshift = bf(r(DO) * 0.3)
    g = bf(r((B, S, DO)) * np.exp2(np.random.randint(-6, 1, (B, S, 1))) / s * u)
    zgate = f64(e) @ f64(Wgate) + f64(bgate)
    zscale = f64(e) @ f64(Wscale) + f64(bscale)
    return {
        "x": bf(f64(x0) * s),
        "edge_features": e,
        "Wv": bf(f64(Wv0) / u),
        "bv": bv,
        "Wgate": Wgate,
        "bgate": bgate,
        "Wscale": Wscale,
        "bscale": bscale,
        "Wshift": Wshift,
        "bshift": bshift,
        "zgate": np.asarray(zgate, np.float32),
        "zscale": np.asarray(zscale, np.float32),
        "grad_out": g,
    }


def reference(x, edge_features, Wv, bv, Wgate, bgate, Wscale, bscale, Wshift, bshift, zgate, zscale, grad_out):
    m = sigmoid(f64(zgate)) * (1.0 + np.tanh(f64(zscale)))
    dv = (f64(grad_out) * m[:, None, :]).reshape(B * S, DO)
    dx = (mxq(dv, 1, "e5m2") @ mxq(f64(Wv), 1, "e4m3").T).reshape(B, S, D)
    dWv = mxq(f64(x).reshape(B * S, D), 0, "e4m3").T @ mxq(dv, 0, "e5m2")
    return dx, dWv

@@ -1,0 +1,287 @@
+from contextlib import ExitStack
+
+import concourse.mybir as mybir
+from concourse.masks import make_identity
+
+F32 = mybir.dt.float32
+BF16 = mybir.dt.bfloat16
+U32 = mybir.dt.uint32
+U8 = mybir.dt.uint8
+E4M3X4 = mybir.dt.float8_e4m3fn_x4
+E5M2X4 = mybir.dt.float8_e5m2_x4
+MULT = mybir.AluOpType.mult
+ADD = mybir.AluOpType.add
+SIGMOID = mybir.ActivationFunctionType.Sigmoid
+
+P = 128
+SAMPLES, ROWS, D, DO = 128, 16, 512, 512
+TOKENS = SAMPLES * ROWS
+GROUPS = 4
+
+FLOPS = 2 * 2 * TOKENS * D * DO
+BYTES = 2 * (2 * TOKENS * 512 + D * DO) + 4 * (2 * SAMPLES * DO + TOKENS * D + D * DO)
+
+
+def tile_graphditunit_pa_v_kernel(
+    tc, x, edge_features, Wv, bv, Wgate, bgate, Wscale, bscale, Wshift, bshift,
+    zgate, zscale, grad_out, out_0, out_1,
+):
+    nc = tc.nc
+    x_hbm = x.rearrange("b s d -> (b s) d").rearrange("(g p t) d -> g p (t d)", p=P, t=4)
+    go_hbm = grad_out.rearrange("b s d -> (b s) d").rearrange("(g p t) d -> g p (t d)", p=P, t=4)
+    w_hbm = Wv.rearrange("(p c) f -> p (c f)", c=4)
+    dx_hbm = out_0.rearrange("b s d -> (b s) d").rearrange("(g p t) d -> g p t d", p=P, t=4)
+
+    with ExitStack() as ctx:
+        keep = ctx.enter_context(tc.tile_pool(name="keep", bufs=1))
+        psum = ctx.enter_context(tc.psum_pool(name="psum", bufs=2))
+
+        def sb(name, shape, dtype):
+            return keep.tile(shape, dtype, name=name, align_bytes=64)
+
+        BANKS = {"m_rep": 2, "dv_bank": 2, "dx_bank": 3, "dw_bank": 1}
+
+        def bank(tag, shape=(P, 512)):
+            return psum.tile(list(shape), F32, name=tag, bufs=BANKS[tag])
+
+        zg = sb("zg", [P, DO], F32)
+        zs = sb("zs", [P, DO], F32)
+        w_raw = sb("w_raw", [P, 4 * DO], BF16)
+        x_raw = [sb("x_raw%d" % g, [P, 4 * D], BF16) for g in range(GROUPS)]
+        go = [sb("go%d" % g, [P, 4 * DO], BF16) for g in range(GROUPS)]
+        warm = sb("warm", [P, 1], F32)
+        ident = sb("ident", [P, P], F32)
+        sel = sb("sel", [P, P, 4], F32)
+        sig_g = sb("sig_g", [P, DO], F32)
+        sig_s = sb("sig_s", [P, DO], F32)
+        m = sb("m", [P, DO], F32)
+        w_sorted = sb("w_sorted", [P, 4 * DO], BF16)
+        w_t = sb("w_t", [P, 4 * D], BF16)
+        w_codes = sb("w_codes", [P, D], U32)
+        w_scales = sb("w_scales", [P, D], U8)
+        xg = [sb("xg%d" % g, [P, 4 * D], BF16) for g in range(GROUPS)]
+        x_codes = [sb("x_codes%d" % g, [P, D], U32) for g in range(GROUPS)]
+        x_scales = [sb("x_scales%d" % g, [P, D], U8) for g in range(GROUPS)]
+        dv = [sb("dv%d" % g, [P, 4, P, 4], BF16) for g in range(GROUPS)]
+        dv_codes = [sb("dv_codes%d" % g, [P, DO], U32) for g in range(GROUPS)]
+        dv_scales = [sb("dv_scales%d" % g, [P, DO], U8) for g in range(GROUPS)]
+        GH = [(g, h) for g in range(GROUPS) for h in range(2)]
+        dvt = {gh: sb("dvt%d%d" % gh, [P, 4 * 256], BF16) for gh in GH}
+        dvt_codes = {gh: sb("dvt_codes%d%d" % gh, [P, 256], U32) for gh in GH}
+        dvt_scales = {gh: sb("dvt_scales%d%d" % gh, [P, 256], U8) for gh in GH}
+        dx = {gh: sb("dx%d%d" % gh, [P, 2, D], F32) for gh in GH}
+        dw = [sb("dw%d" % i, [P, DO], F32) for i in range(4)]
+
+        ctx.enter_context(tc.manual_schedule())
+
+        nc.sync.dma_start(out=zg[:], in_=zgate)
+        nc.scalar.dma_start(out=zs[:], in_=zscale)
+        nc.sync.dma_start(out=w_raw[:], in_=w_hbm)
+        for g in range(GROUPS):
+            nc.sync.dma_start(out=go[g][:], in_=go_hbm[g])
+            nc.sync.dma_start(out=x_raw[g][:], in_=x_hbm[g])
+
+        nc.vector.memset(warm[:], 0.0)
+        nc.scalar.activation(out=warm[:], in_=warm[:], func=SIGMOID)
+        make_identity(nc, ident[:])
+        nc.vector.tensor_copy(out=sel[:], in_=ident[:].unsqueeze(2).to_broadcast([P, P, 4]))
+
+        m_rep = {}
+        dv_bank = {}
+        dx_bank = {}
+        dw_bank = {}
+
+        def spread_m(g, cols=slice(0, DO)):
+            if g not in m_rep:
+                m_rep[g] = bank("m_rep")
+            nc.tensor.matmul(
+                m_rep[g][:, cols], lhsT=sel[:].rearrange("s j c -> s (j c)")[:, g * P : (g + 1) * P], rhs=m[:, cols],
+                start=True, stop=True,
+            )
+
+        def multiply(g, q):
+            nc.vector.tensor_tensor(
+                out=dv[g][:, q].rearrange("p (b r) t -> p b r t", r=8),
+                in0=go[g][:].rearrange("p (t b q r) -> p q b r t", t=4, q=4, r=8)[:, q],
+                in1=m_rep[g][:].rearrange("p (b q r) -> p q b r", q=4, r=8)[:, q].unsqueeze(3).to_broadcast([P, 16, 8, 4]),
+                op=MULT,
+            )
+
+        def quantize_dv(g):
+            nc.vector.quantize_mx(
+                out=dv_codes[g][:].bitcast(E5M2X4), scales=dv_scales[g][:],
+                in_=dv[g][:].rearrange("p q n t -> p (q n t)"),
+            )
+
+        def transpose_dv(g):
+            words = dv[g][:].rearrange("p q n t -> p (q n t)").bitcast(F32)
+            for h in range(2):
+                dv_bank[g, h] = bank("dv_bank", (P, 4, P))
+                for q in range(4):
+                    nc.tensor.transpose(dv_bank[g, h][:, q, :], words[:, q * 256 + h : (q + 1) * 256 : 2], ident[:])
+
+        def copy_dvt(g, h):
+            nc.scalar.copy(
+                out=dvt[g, h][:].rearrange("k (e p q) -> k e p q", e=2, q=4),
+                in_=dv_bank[g, h][:].bitcast(BF16).rearrange("k q (p e) -> k e p q", e=2),
+            )
+
+        def quantize_dvt(g, h):
+            nc.vector.quantize_mx(
+                out=dvt_codes[g, h][:].bitcast(E5M2X4), scales=dvt_scales[g, h][:], in_=dvt[g, h][:],
+            )
+
+        def multiply_dx(g, h):
+            for e in range(2):
+                dx_bank[g, h, e] = bank("dx_bank")
+                cols = slice(e * P, (e + 1) * P)
+                nc.tensor.matmul_mx(
+                    out=dx_bank[g, h, e][:],
+                    lhsT=dvt_codes[g, h][:, cols].bitcast(E5M2X4), lhsT_scale=dvt_scales[g, h][:, cols],
+                    rhs=w_codes[:].bitcast(E4M3X4), rhs_scale=w_scales[:],
+                    start=True, stop=True,
+                )
+
+        def copy_dx(g, h, e, copy):
+            copy(out=dx[g, h][:, e, :], in_=dx_bank[g, h, e][:])
+
+        def store_dx(g, h):
+            nc.sync.dma_start(out=dx_hbm[g][:, 2 * h : 2 * h + 2, :], in_=dx[g, h][:])
+
+        def group_x(g, copy):
+            copy(
+                out=xg[g][:].rearrange("p (c i t) -> p c t i", i=4, t=4),
+                in_=x_raw[g][:].rearrange("p (t c i) -> p c t i", t=4, i=4),
+            )
+
+        def group_x_pool(g):
+            for k in range(4):
+                nc.gpsimd.tensor_scalar(
+                    out=xg[g][:].rearrange("p (k n t) -> p k n t", k=4, t=4)[:, k],
+                    in0=x_raw[g][:].rearrange("p (t k n) -> p k n t", t=4, k=4)[:, k],
+                    scalar1=1.0, scalar2=0.0, op0=MULT, op1=ADD,
+                )
+
+        def quantize_x(g):
+            nc.vector.quantize_mx(out=x_codes[g][:].bitcast(E4M3X4), scales=x_scales[g][:], in_=xg[g][:])
+
+        def multiply_dw(i, g, tag):
+            if g == 0:
+                dw_bank[i] = bank(tag)
+            cols = slice(i * P, (i + 1) * P)
+            nc.tensor.matmul_mx(
+                out=dw_bank[i][:],
+                lhsT=x_codes[g][:, cols].bitcast(E4M3X4), lhsT_scale=x_scales[g][:, cols],
+                rhs=dv_codes[g][:].bitcast(E5M2X4), rhs_scale=dv_scales[g][:],
+                start=(g == 0), stop=(g == GROUPS - 1),
+            )
+
+        def finish_dw(i, copy):
+            copy(
+                out=dw[i][:].rearrange("p (b q r) -> p b q r", q=4, r=8),
+                in_=dw_bank[i][:].rearrange("p (q b r) -> p b q r", q=4, r=8),
+            )
+            nc.sync.dma_start(out=out_1[i * P : (i + 1) * P, :], in_=dw[i][:])
+
+        VC = nc.vector.tensor_copy
+        SC = nc.scalar.copy
+
+        def sort_w(c, u, copy):
+            copy(
+                out=w_sorted[:].rearrange("p (c u b r e) -> p c u b r e", c=4, u=2, r=8, e=2)[:, c, u],
+                in_=w_raw[:].rearrange("p (c b u e r) -> p c u b r e", c=4, u=2, e=2, r=8)[:, c, u],
+            )
+
+        nc.scalar.activation(out=sig_g[:], in_=zg[:], func=SIGMOID)
+        for half in (slice(0, 256), slice(256, 512)):
+            nc.scalar.activation(out=sig_s[:, half], in_=zs[:, half], func=SIGMOID, scale=2.0)
+            nc.vector.scalar_tensor_tensor(
+                out=m[:, half], in0=sig_g[:, half], scalar=2.0, in1=sig_s[:, half], op0=MULT, op1=MULT
+            )
+            spread_m(0, half)
+        spread_m(1)
+        for i in range(8):
+            sort_w(i // 2, i % 2, VC if i in (1, 4) else SC)
+        w_words = w_sorted[:].bitcast(F32)
+        w_bank = [bank("dx_bank", (P, 2, 2, P)) for k in range(2)]
+        for k in range(2):
+            for c in range(2):
+                for u in range(2):
+                    at = (4 * k + 2 * c + u) * P
+                    nc.tensor.transpose(w_bank[k][:, c, u, :], w_words[:, at : at + P], ident[:])
+        for k in range(2):
+            nc.scalar.copy(
+                out=w_t[:].bitcast(F32).rearrange("k (p c u) -> k p c u", c=4, u=2)[:, :, 2 * k : 2 * k + 2, :],
+                in_=w_bank[k][:].rearrange("k c u p -> k p c u"),
+            )
+        for g in range(GROUPS):
+            group_x_pool(g)
+
+        def quantize_w():
+            nc.vector.quantize_mx(out=w_codes[:].bitcast(E4M3X4), scales=w_scales[:], in_=w_t[:])
+
+        for q in range(4):
+            multiply(0, q)
+        transpose_dv(0)
+        quantize_w()
+        spread_m(2)
+        copy_dvt(0, 0)
+        copy_dvt(0, 1)
+        for g in range(3):
+            multiply(g + 1, 0)
+            multiply(g + 1, 1)
+            quantize_dvt(g, 0)
+            multiply_dx(g, 0)
+            multiply(g + 1, 2)
+            multiply(g + 1, 3)
+            transpose_dv(g + 1)
+            copy_dx(g, 0, 0, SC)
+            copy_dx(g, 0, 1, SC)
+            store_dx(g, 0)
+            copy_dvt(g + 1, 0)
+            if g == 2:
+                quantize_dv(2)
+            quantize_dvt(g, 1)
+            multiply_dx(g, 1)
+            if g == 0:
+                spread_m(3)
+            if g < 2:
+                quantize_dv(g)
+            quantize_x(g)
+            for i in range(2):
+                if g > 0 and i == 1:
+                    if g == 1:
+                        multiply_dw(1, 0, "m_rep")
+                    multiply_dw(1, g, "m_rep")
+                if i == 0:
+                    multiply_dw(0, g, "dw_bank")
+            if g < 2:
+                copy_dx(g, 1, 0, SC)
+                copy_dx(g, 1, 1, SC)
+                store_dx(g, 1)
+            copy_dvt(g + 1, 1)
+        for k in range(3):
+            multiply_dw(2, k, "m_rep")
+        quantize_dv(3)
+        quantize_dvt(3, 0)
+        multiply_dx(3, 0)
+        quantize_x(3)
+        copy_dx(2, 1, 0, VC)
+        copy_dx(2, 1, 1, SC)
+        store_dx(2, 1)
+        for i in range(3):
+            multiply_dw(i, 3, "")
+        quantize_dvt(3, 1)
+        for k in range(4):
+            multiply_dw(3, k, "dv_bank")
+        multiply_dx(3, 1)
+        copy_dx(3, 0, 0, SC)
+        finish_dw(0, VC)
+        copy_dx(3, 0, 1, SC)
+        store_dx(3, 0)
+        finish_dw(1, VC)
+        finish_dw(2, SC)
+        finish_dw(3, VC)
+        copy_dx(3, 1, 0, SC)
+        copy_dx(3, 1, 1, VC)
+        store_dx(3, 1)

@@ -77,9 +77,14 @@ def tile_graphditunit_pa_v_kernel(
         nc.sync.dma_start(out=zg[:], in_=zgate)
         nc.scalar.dma_start(out=zs[:], in_=zscale)
         nc.sync.dma_start(out=w_raw[:], in_=w_hbm)
-        for g in range(GROUPS):
-            nc.sync.dma_start(out=go[g][:], in_=go_hbm[g])
-            nc.sync.dma_start(out=x_raw[g][:], in_=x_hbm[g])
+        nc.sync.dma_start(out=go[0][:], in_=go_hbm[0])
+        nc.sync.dma_start(out=x_raw[0][:], in_=x_hbm[0])
+        nc.sync.dma_start(out=go[1][:], in_=go_hbm[1])
+        nc.sync.dma_start(out=x_raw[1][:], in_=x_hbm[1])
+        nc.sync.dma_start(out=go[2][:], in_=go_hbm[2])
+        nc.sync.dma_start(out=x_raw[2][:], in_=x_hbm[2])
+        nc.sync.dma_start(out=go[3][:], in_=go_hbm[3])
+        nc.sync.dma_start(out=x_raw[3][:], in_=x_hbm[3])
 
         nc.vector.memset(warm[:], 0.0)
         nc.scalar.activation(out=warm[:], in_=warm[:], func=SIGMOID)
@@ -192,96 +197,229 @@ def tile_graphditunit_pa_v_kernel(
                 in_=w_raw[:].rearrange("p (c b u e r) -> p c u b r e", c=4, u=2, e=2, r=8)[:, c, u],
             )
 
-        nc.scalar.activation(out=sig_g[:], in_=zg[:], func=SIGMOID)
-        for half in (slice(0, 256), slice(256, 512)):
-            nc.scalar.activation(out=sig_s[:, half], in_=zs[:, half], func=SIGMOID, scale=2.0)
-            nc.vector.scalar_tensor_tensor(
-                out=m[:, half], in0=sig_g[:, half], scalar=2.0, in1=sig_s[:, half], op0=MULT, op1=MULT
-            )
-            spread_m(0, half)
-        spread_m(1)
-        for i in range(8):
-            sort_w(i // 2, i % 2, VC if i in (1, 4) else SC)
         w_words = w_sorted[:].bitcast(F32)
-        w_bank = [bank("dx_bank", (P, 2, 2, P)) for k in range(2)]
-        for k in range(2):
+        w_bank = {}
+
+        def transpose_w(k):
+            w_bank[k] = bank("dx_bank", (P, 2, 2, P))
             for c in range(2):
                 for u in range(2):
                     at = (4 * k + 2 * c + u) * P
                     nc.tensor.transpose(w_bank[k][:, c, u, :], w_words[:, at : at + P], ident[:])
-        for k in range(2):
-            nc.scalar.copy(
+
+        def copy_w(k, copy):
+            copy(
                 out=w_t[:].bitcast(F32).rearrange("k (p c u) -> k p c u", c=4, u=2)[:, :, 2 * k : 2 * k + 2, :],
                 in_=w_bank[k][:].rearrange("k c u p -> k p c u"),
             )
-        for g in range(GROUPS):
-            group_x_pool(g)
 
         def quantize_w():
             nc.vector.quantize_mx(out=w_codes[:].bitcast(E4M3X4), scales=w_scales[:], in_=w_t[:])
 
-        for q in range(4):
-            multiply(0, q)
-        transpose_dv(0)
-        quantize_w()
+        HALF = (slice(0, 256), slice(256, 512))
+
+        def sigmoid_scale(h):
+            nc.scalar.activation(out=sig_s[:, HALF[h]], in_=zs[:, HALF[h]], func=SIGMOID, scale=2.0)
+
+        def make_m(h):
+            nc.vector.scalar_tensor_tensor(
+                out=m[:, HALF[h]], in0=sig_g[:, HALF[h]], scalar=2.0, in1=sig_s[:, HALF[h]], op0=MULT, op1=MULT
+            )
+
+        def transpose_half(g, h):
+            words = dv[g][:].rearrange("p q n t -> p (q n t)").bitcast(F32)
+            dv_bank[g, h] = bank("dv_bank", (P, 4, P))
+            for q in range(4):
+                nc.tensor.transpose(dv_bank[g, h][:, q, :], words[:, q * 256 + h : (q + 1) * 256 : 2], ident[:])
+
+        def copy_dvt_by(g, h, copy):
+            copy(
+                out=dvt[g, h][:].rearrange("k (e p q) -> k e p q", e=2, q=4),
+                in_=dv_bank[g, h][:].bitcast(BF16).rearrange("k q (p e) -> k e p q", e=2),
+            )
+
+        def mx_dx(g, t):
+            h, e = t // 2, t % 2
+            dx_bank[g, h, e] = bank("dx_bank")
+            cols = slice(e * P, (e + 1) * P)
+            nc.tensor.matmul_mx(
+                out=dx_bank[g, h, e][:],
+                lhsT=dvt_codes[g, h][:, cols].bitcast(E5M2X4), lhsT_scale=dvt_scales[g, h][:, cols],
+                rhs=w_codes[:].bitcast(E4M3X4), rhs_scale=w_scales[:],
+                start=True, stop=True,
+            )
+
+        def store_row(g, t):
+            nc.sync.dma_start(out=dx_hbm[g][:, t, :], in_=dx[g, t // 2][:, t % 2, :])
+
+        def x_half(g, j, copy):
+            copy(
+                out=xg[g][:].rearrange("p (j c i t) -> p j c t i", j=2, i=4, t=4)[:, j],
+                in_=x_raw[g][:].rearrange("p (t j c i) -> p j c t i", t=4, j=2, i=4)[:, j],
+            )
+
+        def x_quarter(g, k):
+            nc.gpsimd.tensor_scalar(
+                out=xg[g][:].rearrange("p (k n t) -> p k n t", k=4, t=4)[:, k],
+                in0=x_raw[g][:].rearrange("p (t k n) -> p k n t", t=4, k=4)[:, k],
+                scalar1=1.0, scalar2=0.0, op0=MULT, op1=ADD,
+            )
+
+        def copy_dw(i, copy):
+            copy(
+                out=dw[i][:].rearrange("p (b q r) -> p b q r", q=4, r=8),
+                in_=dw_bank[i][:].rearrange("p (q b r) -> p b q r", q=4, r=8),
+            )
+
+        def store_dw(i):
+            nc.sync.dma_start(out=out_1[i * P : (i + 1) * P, :], in_=dw[i][:])
+
+        nc.scalar.activation(out=sig_g[:], in_=zg[:], func=SIGMOID)
+        sigmoid_scale(0)
+        make_m(0)
+        spread_m(0, HALF[0])
+        sigmoid_scale(1)
+        make_m(1)
+        spread_m(0, HALF[1])
+        sort_w(0, 0, SC)
+        sort_w(0, 1, SC)
+        sort_w(1, 0, VC)
+        sort_w(1, 1, VC)
+        sort_w(2, 0, VC)
+        sort_w(2, 1, VC)
+        sort_w(3, 0, VC)
+        sort_w(3, 1, VC)
+        spread_m(1)
+        transpose_w(0)
+        copy_w(0, SC)
+        transpose_w(1)
+        copy_w(1, SC)
+        multiply(0, 3)
         spread_m(2)
-        copy_dvt(0, 0)
-        copy_dvt(0, 1)
-        for g in range(3):
-            multiply(g + 1, 0)
-            multiply(g + 1, 1)
-            quantize_dvt(g, 0)
-            multiply_dx(g, 0)
-            multiply(g + 1, 2)
-            multiply(g + 1, 3)
-            transpose_dv(g + 1)
-            copy_dx(g, 0, 0, SC)
-            copy_dx(g, 0, 1, SC)
-            store_dx(g, 0)
-            copy_dvt(g + 1, 0)
-            if g == 2:
-                quantize_dv(2)
-            quantize_dvt(g, 1)
-            multiply_dx(g, 1)
-            if g == 0:
-                spread_m(3)
-            if g < 2:
-                quantize_dv(g)
-            quantize_x(g)
-            for i in range(2):
-                if g > 0 and i == 1:
-                    if g == 1:
-                        multiply_dw(1, 0, "m_rep")
-                    multiply_dw(1, g, "m_rep")
-                if i == 0:
-                    multiply_dw(0, g, "dw_bank")
-            if g < 2:
-                copy_dx(g, 1, 0, SC)
-                copy_dx(g, 1, 1, SC)
-                store_dx(g, 1)
-            copy_dvt(g + 1, 1)
-        for k in range(3):
-            multiply_dw(2, k, "m_rep")
-        quantize_dv(3)
-        quantize_dvt(3, 0)
-        multiply_dx(3, 0)
-        quantize_x(3)
-        copy_dx(2, 1, 0, VC)
+        multiply(0, 0)
+        multiply(0, 2)
+        multiply(0, 1)
+        transpose_half(0, 0)
+        copy_dvt_by(0, 0, SC)
+        transpose_half(0, 1)
+        copy_dvt_by(0, 1, SC)
+        multiply(1, 3)
+        spread_m(3)
+        multiply(1, 0)
+        multiply(1, 2)
+        x_quarter(0, 0)
+        x_quarter(0, 1)
+        x_quarter(0, 2)
+        x_quarter(0, 3)
+        multiply(1, 1)
+        transpose_half(1, 0)
+        copy_dvt_by(1, 0, SC)
+        transpose_half(1, 1)
+        copy_dvt_by(1, 1, SC)
+        multiply(2, 3)
+        multiply(2, 0)
+        multiply(2, 2)
+        x_quarter(1, 0)
+        x_quarter(1, 1)
+        x_quarter(1, 2)
+        x_quarter(1, 3)
+        multiply(2, 1)
+        transpose_half(2, 0)
+        copy_dvt_by(2, 0, SC)
+        transpose_half(2, 1)
+        copy_dvt_by(2, 1, SC)
+        quantize_w()
+        quantize_dvt(0, 0)
+        mx_dx(0, 0)
+        mx_dx(0, 1)
+        quantize_dvt(0, 1)
+        multiply(3, 2)
+        multiply(3, 3)
+        x_quarter(2, 0)
+        x_quarter(2, 1)
+        x_quarter(2, 2)
+        x_quarter(2, 3)
+        copy_dx(0, 0, 0, SC)
+        multiply(3, 0)
+        copy_dx(0, 0, 1, SC)
+        store_dx(0, 0)
+        mx_dx(0, 2)
+        copy_dx(0, 1, 0, VC)
+        mx_dx(0, 3)
+        copy_dx(0, 1, 1, SC)
+        store_dx(0, 1)
+        multiply(3, 1)
+        transpose_half(3, 0)
+        copy_dvt_by(3, 0, SC)
+        transpose_half(3, 1)
+        copy_dvt_by(3, 1, SC)
+        quantize_dvt(1, 0)
+        mx_dx(1, 0)
+        mx_dx(1, 1)
+        x_half(3, 0, VC)
+        x_half(3, 1, VC)
+        quantize_dvt(1, 1)
+        copy_dx(1, 0, 0, VC)
+        copy_dx(1, 0, 1, VC)
+        store_dx(1, 0)
+        mx_dx(1, 2)
+        copy_dx(1, 1, 0, SC)
+        mx_dx(1, 3)
+        copy_dx(1, 1, 1, SC)
+        store_dx(1, 1)
+        quantize_dvt(2, 0)
+        mx_dx(2, 0)
+        mx_dx(2, 1)
+        quantize_dvt(2, 1)
+        copy_dx(2, 0, 0, SC)
+        quantize_dv(0)
+        copy_dx(2, 0, 1, SC)
+        store_dx(2, 0)
+        mx_dx(2, 2)
+        copy_dx(2, 1, 0, SC)
+        mx_dx(2, 3)
         copy_dx(2, 1, 1, SC)
         store_dx(2, 1)
-        for i in range(3):
-            multiply_dw(i, 3, "")
-        quantize_dvt(3, 1)
-        for k in range(4):
-            multiply_dw(3, k, "dv_bank")
-        multiply_dx(3, 1)
+        quantize_x(0)
+        multiply_dw(2, 0, "m_rep")
+        multiply_dw(0, 0, "dw_bank")
+        quantize_dvt(3, 0)
+        mx_dx(3, 0)
+        mx_dx(3, 1)
         copy_dx(3, 0, 0, SC)
-        finish_dw(0, VC)
+        quantize_dvt(3, 1)
+        multiply_dw(1, 0, "m_rep")
+        quantize_dv(1)
+        quantize_x(1)
+        multiply_dw(2, 1, "m_rep")
         copy_dx(3, 0, 1, SC)
         store_dx(3, 0)
-        finish_dw(1, VC)
-        finish_dw(2, SC)
-        finish_dw(3, VC)
+        mx_dx(3, 2)
         copy_dx(3, 1, 0, SC)
-        copy_dx(3, 1, 1, VC)
+        mx_dx(3, 3)
+        copy_dx(3, 1, 1, SC)
         store_dx(3, 1)
+        multiply_dw(0, 1, "dw_bank")
+        multiply_dw(1, 1, "m_rep")
+        quantize_dv(2)
+        quantize_x(2)
+        multiply_dw(2, 2, "m_rep")
+        multiply_dw(0, 2, "dw_bank")
+        multiply_dw(1, 2, "m_rep")
+        quantize_dv(3)
+        quantize_x(3)
+        multiply_dw(2, 3, "m_rep")
+        copy_dw(2, VC)
+        store_dw(2)
+        multiply_dw(0, 3, "dw_bank")
+        copy_dw(0, VC)
+        store_dw(0)
+        multiply_dw(1, 3, "m_rep")
+        copy_dw(1, VC)
+        store_dw(1)
+        multiply_dw(3, 0, "dv_bank")
+        multiply_dw(3, 1, "dv_bank")
+        multiply_dw(3, 2, "dv_bank")
+        multiply_dw(3, 3, "dv_bank")
+        copy_dw(3, VC)
+        store_dw(3)

@@ -106,9 +106,9 @@ def tile_graphditunit_pa_v_kernel(
 
         def multiply(g, q):
             nc.vector.tensor_tensor(
-                out=dv[g][:, q].rearrange("p (b r) t -> p b r t", r=8),
-                in0=go[g][:].rearrange("p (t b q r) -> p q b r t", t=4, q=4, r=8)[:, q],
-                in1=m_rep[g][:].rearrange("p (b q r) -> p q b r", q=4, r=8)[:, q].unsqueeze(3).to_broadcast([P, 16, 8, 4]),
+                out=dv[g][:, q].rearrange("p (b r) t -> p b t r", r=8),
+                in0=go[g][:].rearrange("p (t b q r) -> p q b t r", t=4, q=4, r=8)[:, q],
+                in1=m_rep[g][:].rearrange("p (b q r) -> p q b r", q=4, r=8)[:, q].unsqueeze(2).to_broadcast([P, 16, 4, 8]),
                 op=MULT,
             )
 

@@ -33,6 +33,7 @@ def tile_graphditunit_pa_v_kernel(
     dx_hbm = out_0.rearrange("b s d -> (b s) d").rearrange("(g p t) d -> g p t d", p=P, t=4)
 
     with ExitStack() as ctx:
+        HALF = (slice(0, 256), slice(256, 512))
         keep = ctx.enter_context(tc.tile_pool(name="keep", bufs=1))
         psum = ctx.enter_context(tc.psum_pool(name="psum", bufs=2))
 
@@ -50,6 +51,7 @@ def tile_graphditunit_pa_v_kernel(
         x_raw = [sb("x_raw%d" % g, [P, 4 * D], BF16) for g in range(GROUPS)]
         go = [sb("go%d" % g, [P, 4 * DO], BF16) for g in range(GROUPS)]
         warm = sb("warm", [P, 1], F32)
+        idle = sb("idle", [P, P], F32)
         ident = sb("ident", [P, P], F32)
         sel = sb("sel", [P, P, 4], F32)
         sig_g = sb("sig_g", [P, DO], F32)
@@ -74,10 +76,11 @@ def tile_graphditunit_pa_v_kernel(
 
         ctx.enter_context(tc.manual_schedule())
 
-        nc.sync.dma_start(out=zg[:], in_=zgate)
-        nc.scalar.dma_start(out=zs[:], in_=zscale)
-        nc.sync.dma_start(out=w_raw[:], in_=w_hbm)
+        for half in HALF:
+            nc.sync.dma_start(out=zg[:, half], in_=zgate[:, half])
+            nc.scalar.dma_start(out=zs[:, half], in_=zscale[:, half])
         nc.sync.dma_start(out=go[0][:], in_=go_hbm[0])
+        nc.sync.dma_start(out=w_raw[:], in_=w_hbm)
         nc.sync.dma_start(out=x_raw[0][:], in_=x_hbm[0])
         nc.sync.dma_start(out=go[1][:], in_=go_hbm[1])
         nc.sync.dma_start(out=x_raw[1][:], in_=x_hbm[1])
@@ -87,6 +90,7 @@ def tile_graphditunit_pa_v_kernel(
         nc.sync.dma_start(out=x_raw[3][:], in_=x_hbm[3])
 
         nc.vector.memset(warm[:], 0.0)
+        nc.vector.memset(idle[:], 0.0)
         nc.scalar.activation(out=warm[:], in_=warm[:], func=SIGMOID)
         make_identity(nc, ident[:])
         nc.vector.tensor_copy(out=sel[:], in_=ident[:].unsqueeze(2).to_broadcast([P, P, 4]))
@@ -216,7 +220,8 @@ def tile_graphditunit_pa_v_kernel(
         def quantize_w():
             nc.vector.quantize_mx(out=w_codes[:].bitcast(E4M3X4), scales=w_scales[:], in_=w_t[:])
 
-        HALF = (slice(0, 256), slice(256, 512))
+        def sigmoid_gate(h):
+            nc.scalar.activation(out=sig_g[:, HALF[h]], in_=zg[:, HALF[h]], func=SIGMOID)
 
         def sigmoid_scale(h):
             nc.scalar.activation(out=sig_s[:, HALF[h]], in_=zs[:, HALF[h]], func=SIGMOID, scale=2.0)
@@ -226,9 +231,21 @@ def tile_graphditunit_pa_v_kernel(
                 out=m[:, HALF[h]], in0=sig_g[:, HALF[h]], scalar=2.0, in1=sig_s[:, HALF[h]], op0=MULT, op1=MULT
             )
 
+        def tick(tile):
+            nc.tensor.matmul(tile, lhsT=idle[:], rhs=idle[:], start=True, stop=True)
+
+        def tick_dv(g, h):
+            dv_bank[g, h] = bank("dv_bank", (P, 4, P))
+            tick(dv_bank[g, h][:, 0, :])
+
+        def tick_dx(g, t):
+            dx_bank[g, t // 2, t % 2] = bank("dx_bank")
+            tick(dx_bank[g, t // 2, t % 2][:, :P])
+
         def transpose_half(g, h):
             words = dv[g][:].rearrange("p q n t -> p (q n t)").bitcast(F32)
-            dv_bank[g, h] = bank("dv_bank", (P, 4, P))
+            if (g, h) not in dv_bank:
+                dv_bank[g, h] = bank("dv_bank", (P, 4, P))
             for q in range(4):
                 nc.tensor.transpose(dv_bank[g, h][:, q, :], words[:, q * 256 + h : (q + 1) * 256 : 2], ident[:])
 
@@ -240,7 +257,8 @@ def tile_graphditunit_pa_v_kernel(
 
         def mx_dx(g, t):
             h, e = t // 2, t % 2
-            dx_bank[g, h, e] = bank("dx_bank")
+            if (g, h, e) not in dx_bank:
+                dx_bank[g, h, e] = bank("dx_bank")
             cols = slice(e * P, (e + 1) * P)
             nc.tensor.matmul_mx(
                 out=dx_bank[g, h, e][:],
@@ -274,152 +292,166 @@ def tile_graphditunit_pa_v_kernel(
         def store_dw(i):
             nc.sync.dma_start(out=out_1[i * P : (i + 1) * P, :], in_=dw[i][:])
 
-        nc.scalar.activation(out=sig_g[:], in_=zg[:], func=SIGMOID)
+        warm_bank = bank("dw_bank")
+        tick(warm_bank[:, :P])
+        tick(warm_bank[:, :P])
+        tick(warm_bank[:, :P])
+        tick(warm_bank[:, :P])
+        sigmoid_gate(0)
+        tick(warm_bank[:, :P])
         sigmoid_scale(0)
-        make_m(0)
-        spread_m(0, HALF[0])
         sigmoid_scale(1)
+        make_m(0)
+        sigmoid_gate(1)
+        spread_m(0, HALF[0])
         make_m(1)
         spread_m(0, HALF[1])
-        sort_w(0, 0, SC)
-        sort_w(0, 1, SC)
-        sort_w(1, 0, VC)
-        sort_w(1, 1, VC)
-        sort_w(2, 0, VC)
-        sort_w(2, 1, VC)
-        sort_w(3, 0, VC)
-        sort_w(3, 1, VC)
         spread_m(1)
-        transpose_w(0)
-        copy_w(0, SC)
+        sort_w(3, 0, SC)
+        multiply(0, 0)
+        sort_w(2, 1, SC)
+        sort_w(3, 1, SC)
+        multiply(0, 1)
+        sort_w(2, 0, SC)
+        x_quarter(0, 2)
+        multiply(0, 2)
+        sort_w(0, 1, SC)
         transpose_w(1)
-        copy_w(1, SC)
+        sort_w(1, 1, SC)
+        x_quarter(0, 1)
         multiply(0, 3)
         spread_m(2)
-        multiply(0, 0)
-        multiply(0, 2)
-        multiply(0, 1)
-        transpose_half(0, 0)
-        copy_dvt_by(0, 0, SC)
-        transpose_half(0, 1)
-        copy_dvt_by(0, 1, SC)
-        multiply(1, 3)
-        spread_m(3)
+        sort_w(0, 0, SC)
+        sort_w(1, 0, SC)
         multiply(1, 0)
-        multiply(1, 2)
-        x_quarter(0, 0)
-        x_quarter(0, 1)
-        x_quarter(0, 2)
-        x_quarter(0, 3)
+        copy_w(1, SC)
         multiply(1, 1)
+        transpose_w(0)
+        x_quarter(1, 0)
+        transpose_half(0, 1)
+        multiply(1, 2)
+        copy_w(0, SC)
+        transpose_half(0, 0)
+        x_quarter(1, 3)
+        multiply(1, 3)
+        copy_dvt_by(0, 1, SC)
+        spread_m(3)
+        x_quarter(1, 2)
+        multiply(2, 0)
+        x_quarter(0, 3)
+        copy_dvt_by(0, 0, SC)
+        multiply(2, 1)
         transpose_half(1, 0)
+        x_quarter(2, 0)
+        multiply(2, 2)
+        tick_dx(0, 1)
         copy_dvt_by(1, 0, SC)
         transpose_half(1, 1)
-        copy_dvt_by(1, 1, SC)
-        multiply(2, 3)
-        multiply(2, 0)
-        multiply(2, 2)
-        x_quarter(1, 0)
-        x_quarter(1, 1)
-        x_quarter(1, 2)
-        x_quarter(1, 3)
-        multiply(2, 1)
-        transpose_half(2, 0)
-        copy_dvt_by(2, 0, SC)
-        transpose_half(2, 1)
-        copy_dvt_by(2, 1, SC)
         quantize_w()
+        tick_dx(0, 0)
         quantize_dvt(0, 0)
-        mx_dx(0, 0)
-        mx_dx(0, 1)
-        quantize_dvt(0, 1)
-        multiply(3, 2)
-        multiply(3, 3)
-        x_quarter(2, 0)
-        x_quarter(2, 1)
-        x_quarter(2, 2)
+        multiply(2, 3)
         x_quarter(2, 3)
-        copy_dx(0, 0, 0, SC)
+        copy_dvt_by(1, 1, SC)
+        mx_dx(0, 1)
         multiply(3, 0)
+        tick_dv(2, 0)
+        x_quarter(1, 1)
+        mx_dx(0, 0)
         copy_dx(0, 0, 1, SC)
-        store_dx(0, 0)
-        mx_dx(0, 2)
-        copy_dx(0, 1, 0, VC)
-        mx_dx(0, 3)
-        copy_dx(0, 1, 1, SC)
-        store_dx(0, 1)
-        multiply(3, 1)
-        transpose_half(3, 0)
-        copy_dvt_by(3, 0, SC)
-        transpose_half(3, 1)
-        copy_dvt_by(3, 1, SC)
-        quantize_dvt(1, 0)
-        mx_dx(1, 0)
-        mx_dx(1, 1)
-        x_half(3, 0, VC)
-        x_half(3, 1, VC)
+        transpose_half(2, 0)
+        quantize_dvt(0, 1)
         quantize_dvt(1, 1)
-        copy_dx(1, 0, 0, VC)
-        copy_dx(1, 0, 1, VC)
-        store_dx(1, 0)
+        copy_dx(0, 0, 0, SC)
+        tick_dx(1, 2)
+        multiply(3, 1)
+        x_quarter(2, 2)
+        tick_dx(1, 3)
+        copy_dvt_by(2, 0, SC)
         mx_dx(1, 2)
-        copy_dx(1, 1, 0, SC)
+        multiply(3, 2)
+        x_quarter(0, 0)
         mx_dx(1, 3)
-        copy_dx(1, 1, 1, SC)
+        mx_dx(0, 3)
+        multiply(3, 3)
+        transpose_half(2, 1)
+        x_quarter(2, 1)
+        copy_dx(1, 1, 0, SC)
+        copy_dx(1, 1, 1, VC)
+        copy_dx(0, 1, 1, SC)
+        tick_dx(0, 2)
+        mx_dx(0, 2)
+        quantize_dvt(1, 0)
+        copy_dvt_by(2, 1, SC)
         store_dx(1, 1)
-        quantize_dvt(2, 0)
-        mx_dx(2, 0)
-        mx_dx(2, 1)
-        quantize_dvt(2, 1)
-        copy_dx(2, 0, 0, SC)
-        quantize_dv(0)
-        copy_dx(2, 0, 1, SC)
-        store_dx(2, 0)
-        mx_dx(2, 2)
-        copy_dx(2, 1, 0, SC)
-        mx_dx(2, 3)
-        copy_dx(2, 1, 1, SC)
-        store_dx(2, 1)
-        quantize_x(0)
-        multiply_dw(2, 0, "m_rep")
-        multiply_dw(0, 0, "dw_bank")
-        quantize_dvt(3, 0)
-        mx_dx(3, 0)
-        mx_dx(3, 1)
-        copy_dx(3, 0, 0, SC)
-        quantize_dvt(3, 1)
-        multiply_dw(1, 0, "m_rep")
         quantize_dv(1)
+        mx_dx(1, 1)
+        transpose_half(3, 0)
+        quantize_x(0)
+        copy_dx(0, 1, 0, SC)
+        tick_dv(3, 1)
+        quantize_dvt(2, 0)
+        transpose_half(3, 1)
+        copy_dvt_by(3, 0, SC)
         quantize_x(1)
-        multiply_dw(2, 1, "m_rep")
-        copy_dx(3, 0, 1, SC)
-        store_dx(3, 0)
-        mx_dx(3, 2)
-        copy_dx(3, 1, 0, SC)
-        mx_dx(3, 3)
-        copy_dx(3, 1, 1, SC)
-        store_dx(3, 1)
-        multiply_dw(0, 1, "dw_bank")
-        multiply_dw(1, 1, "m_rep")
-        quantize_dv(2)
+        store_dx(0, 1)
+        mx_dx(2, 0)
+        store_dx(0, 0)
+        quantize_dvt(2, 1)
+        mx_dx(1, 0)
+        quantize_dv(0)
+        copy_dx(1, 0, 1, SC)
+        x_half(3, 1, VC)
+        copy_dx(2, 0, 0, SC)
+        mx_dx(2, 2)
+        multiply_dw(0, 0, "dw_bank")
+        copy_dx(1, 0, 0, SC)
         quantize_x(2)
-        multiply_dw(2, 2, "m_rep")
-        multiply_dw(0, 2, "dw_bank")
-        multiply_dw(1, 2, "m_rep")
-        quantize_dv(3)
-        quantize_x(3)
-        multiply_dw(2, 3, "m_rep")
-        copy_dw(2, VC)
-        store_dw(2)
-        multiply_dw(0, 3, "dw_bank")
-        copy_dw(0, VC)
-        store_dw(0)
-        multiply_dw(1, 3, "m_rep")
-        copy_dw(1, VC)
-        store_dw(1)
+        mx_dx(2, 1)
         multiply_dw(3, 0, "dv_bank")
+        copy_dvt_by(3, 1, SC)
+        quantize_dvt(3, 0)
+        multiply_dw(0, 1, "dw_bank")
+        store_dx(1, 0)
+        multiply_dw(2, 0, "m_rep")
+        copy_dx(2, 0, 1, VC)
+        mx_dx(2, 3)
+        multiply_dw(1, 0, "m_rep")
+        quantize_dv(2)
+        copy_dx(2, 1, 0, SC)
+        mx_dx(3, 0)
+        store_dx(2, 0)
         multiply_dw(3, 1, "dv_bank")
+        quantize_dvt(3, 1)
+        copy_dx(2, 1, 1, SC)
+        mx_dx(3, 1)
+        x_half(3, 0, VC)
+        multiply_dw(2, 1, "m_rep")
+        copy_dx(3, 0, 0, SC)
+        multiply_dw(2, 2, "m_rep")
+        store_dx(2, 1)
+        mx_dx(3, 2)
+        quantize_dv(3)
+        copy_dx(3, 0, 1, SC)
+        mx_dx(3, 3)
+        multiply_dw(0, 2, "dw_bank")
+        quantize_x(3)
+        copy_dx(3, 1, 0, SC)
+        store_dx(3, 0)
+        copy_dx(3, 1, 1, VC)
+        multiply_dw(2, 3, "m_rep")
+        multiply_dw(0, 3, "dw_bank")
+        multiply_dw(1, 1, "m_rep")
+        copy_dw(2, VC)
+        store_dx(3, 1)
         multiply_dw(3, 2, "dv_bank")
         multiply_dw(3, 3, "dv_bank")
+        copy_dw(0, VC)
+        multiply_dw(1, 2, "m_rep")
+        store_dw(2)
+        multiply_dw(1, 3, "m_rep")
         copy_dw(3, VC)
+        store_dw(0)
+        copy_dw(1, VC)
         store_dw(3)
+        store_dw(1)

from contextlib import ExitStack

import concourse.mybir as mybir
from concourse.masks import make_identity

F32 = mybir.dt.float32
BF16 = mybir.dt.bfloat16
U32 = mybir.dt.uint32
U8 = mybir.dt.uint8
E4M3X4 = mybir.dt.float8_e4m3fn_x4
E5M2X4 = mybir.dt.float8_e5m2_x4
MULT = mybir.AluOpType.mult
ADD = mybir.AluOpType.add
SIGMOID = mybir.ActivationFunctionType.Sigmoid

P = 128
SAMPLES, ROWS, D, DO = 128, 16, 512, 512
TOKENS = SAMPLES * ROWS
GROUPS = 4

FLOPS = 2 * 2 * TOKENS * D * DO
BYTES = 2 * (2 * TOKENS * 512 + D * DO) + 4 * (2 * SAMPLES * DO + TOKENS * D + D * DO)


def tile_graphditunit_pa_v_kernel(
    tc, x, edge_features, Wv, bv, Wgate, bgate, Wscale, bscale, Wshift, bshift,
    zgate, zscale, grad_out, out_0, out_1,
):
    nc = tc.nc
    x_hbm = x.rearrange("b s d -> (b s) d").rearrange("(g p t) d -> g p (t d)", p=P, t=4)
    go_hbm = grad_out.rearrange("b s d -> (b s) d").rearrange("(g p t) d -> g p (t d)", p=P, t=4)
    w_hbm = Wv.rearrange("(p c) f -> p (c f)", c=4)
    dx_hbm = out_0.rearrange("b s d -> (b s) d").rearrange("(g p t) d -> g p t d", p=P, t=4)

    with ExitStack() as ctx:
        HALF = (slice(0, 256), slice(256, 512))
        keep = ctx.enter_context(tc.tile_pool(name="keep", bufs=1))
        psum = ctx.enter_context(tc.psum_pool(name="psum", bufs=2))

        def sb(name, shape, dtype):
            return keep.tile(shape, dtype, name=name, align_bytes=64)

        BANKS = {"m_rep": 2, "dv_bank": 2, "dx_bank": 3, "dw_bank": 1}

        def bank(tag, shape=(P, 512)):
            return psum.tile(list(shape), F32, name=tag, bufs=BANKS[tag])

        zg = sb("zg", [P, DO], F32)
        zs = sb("zs", [P, DO], F32)
        w_raw = sb("w_raw", [P, 4 * DO], BF16)
        x_raw = [sb("x_raw%d" % g, [P, 4 * D], BF16) for g in range(GROUPS)]
        go = [sb("go%d" % g, [P, 4 * DO], BF16) for g in range(GROUPS)]
        warm = sb("warm", [P, 1], F32)
        idle = sb("idle", [P, P], F32)
        ident = sb("ident", [P, P], F32)
        sel = sb("sel", [P, P, 4], F32)
        sig_g = sb("sig_g", [P, DO], F32)
        sig_s = sb("sig_s", [P, DO], F32)
        m = sb("m", [P, DO], F32)
        w_sorted = sb("w_sorted", [P, 4 * DO], BF16)
        w_t = sb("w_t", [P, 4 * D], BF16)
        w_codes = sb("w_codes", [P, D], U32)
        w_scales = sb("w_scales", [P, D], U8)
        xg = [sb("xg%d" % g, [P, 4 * D], BF16) for g in range(GROUPS)]
        x_codes = [sb("x_codes%d" % g, [P, D], U32) for g in range(GROUPS)]
        x_scales = [sb("x_scales%d" % g, [P, D], U8) for g in range(GROUPS)]
        dv = [sb("dv%d" % g, [P, 4, P, 4], BF16) for g in range(GROUPS)]
        dv_codes = [sb("dv_codes%d" % g, [P, DO], U32) for g in range(GROUPS)]
        dv_scales = [sb("dv_scales%d" % g, [P, DO], U8) for g in range(GROUPS)]
        GH = [(g, h) for g in range(GROUPS) for h in range(2)]
        dvt = {gh: sb("dvt%d%d" % gh, [P, 4 * 256], BF16) for gh in GH}
        dvt_codes = {gh: sb("dvt_codes%d%d" % gh, [P, 256], U32) for gh in GH}
        dvt_scales = {gh: sb("dvt_scales%d%d" % gh, [P, 256], U8) for gh in GH}
        dx = {gh: sb("dx%d%d" % gh, [P, 2, D], F32) for gh in GH}
        dw = [sb("dw%d" % i, [P, DO], F32) for i in range(4)]

        ctx.enter_context(tc.manual_schedule())

        for half in HALF:
            nc.sync.dma_start(out=zg[:, half], in_=zgate[:, half])
            nc.scalar.dma_start(out=zs[:, half], in_=zscale[:, half])
        nc.sync.dma_start(out=go[0][:], in_=go_hbm[0])
        nc.sync.dma_start(out=w_raw[:], in_=w_hbm)
        nc.sync.dma_start(out=x_raw[0][:], in_=x_hbm[0])
        nc.sync.dma_start(out=go[1][:], in_=go_hbm[1])
        nc.sync.dma_start(out=x_raw[1][:], in_=x_hbm[1])
        nc.sync.dma_start(out=go[2][:], in_=go_hbm[2])
        nc.sync.dma_start(out=x_raw[2][:], in_=x_hbm[2])
        nc.sync.dma_start(out=go[3][:], in_=go_hbm[3])
        nc.sync.dma_start(out=x_raw[3][:], in_=x_hbm[3])

        nc.vector.memset(warm[:], 0.0)
        nc.vector.memset(idle[:], 0.0)
        nc.scalar.activation(out=warm[:], in_=warm[:], func=SIGMOID)
        make_identity(nc, ident[:])
        nc.vector.tensor_copy(out=sel[:], in_=ident[:].unsqueeze(2).to_broadcast([P, P, 4]))

        m_rep = {}
        dv_bank = {}
        dx_bank = {}
        dw_bank = {}

        def spread_m(g, cols=slice(0, DO)):
            if g not in m_rep:
                m_rep[g] = bank("m_rep")
            nc.tensor.matmul(
                m_rep[g][:, cols], lhsT=sel[:].rearrange("s j c -> s (j c)")[:, g * P : (g + 1) * P], rhs=m[:, cols],
                start=True, stop=True,
            )

        def multiply(g, q):
            nc.vector.tensor_tensor(
                out=dv[g][:, q].rearrange("p (b r) t -> p b t r", r=8),
                in0=go[g][:].rearrange("p (t b q r) -> p q b t r", t=4, q=4, r=8)[:, q],
                in1=m_rep[g][:].rearrange("p (b q r) -> p q b r", q=4, r=8)[:, q].unsqueeze(2).to_broadcast([P, 16, 4, 8]),
                op=MULT,
            )

        def quantize_dv(g):
            nc.vector.quantize_mx(
                out=dv_codes[g][:].bitcast(E5M2X4), scales=dv_scales[g][:],
                in_=dv[g][:].rearrange("p q n t -> p (q n t)"),
            )

        def transpose_dv(g):
            words = dv[g][:].rearrange("p q n t -> p (q n t)").bitcast(F32)
            for h in range(2):
                dv_bank[g, h] = bank("dv_bank", (P, 4, P))
                for q in range(4):
                    nc.tensor.transpose(dv_bank[g, h][:, q, :], words[:, q * 256 + h : (q + 1) * 256 : 2], ident[:])

        def copy_dvt(g, h):
            nc.scalar.copy(
                out=dvt[g, h][:].rearrange("k (e p q) -> k e p q", e=2, q=4),
                in_=dv_bank[g, h][:].bitcast(BF16).rearrange("k q (p e) -> k e p q", e=2),
            )

        def quantize_dvt(g, h):
            nc.vector.quantize_mx(
                out=dvt_codes[g, h][:].bitcast(E5M2X4), scales=dvt_scales[g, h][:], in_=dvt[g, h][:],
            )

        def multiply_dx(g, h):
            for e in range(2):
                dx_bank[g, h, e] = bank("dx_bank")
                cols = slice(e * P, (e + 1) * P)
                nc.tensor.matmul_mx(
                    out=dx_bank[g, h, e][:],
                    lhsT=dvt_codes[g, h][:, cols].bitcast(E5M2X4), lhsT_scale=dvt_scales[g, h][:, cols],
                    rhs=w_codes[:].bitcast(E4M3X4), rhs_scale=w_scales[:],
                    start=True, stop=True,
                )

        def copy_dx(g, h, e, copy):
            copy(out=dx[g, h][:, e, :], in_=dx_bank[g, h, e][:])

        def store_dx(g, h):
            nc.sync.dma_start(out=dx_hbm[g][:, 2 * h : 2 * h + 2, :], in_=dx[g, h][:])

        def group_x(g, copy):
            copy(
                out=xg[g][:].rearrange("p (c i t) -> p c t i", i=4, t=4),
                in_=x_raw[g][:].rearrange("p (t c i) -> p c t i", t=4, i=4),
            )

        def group_x_pool(g):
            for k in range(4):
                nc.gpsimd.tensor_scalar(
                    out=xg[g][:].rearrange("p (k n t) -> p k n t", k=4, t=4)[:, k],
                    in0=x_raw[g][:].rearrange("p (t k n) -> p k n t", t=4, k=4)[:, k],
                    scalar1=1.0, scalar2=0.0, op0=MULT, op1=ADD,
                )

        def quantize_x(g):
            nc.vector.quantize_mx(out=x_codes[g][:].bitcast(E4M3X4), scales=x_scales[g][:], in_=xg[g][:])

        def multiply_dw(i, g, tag):
            if g == 0:
                dw_bank[i] = bank(tag)
            cols = slice(i * P, (i + 1) * P)
            nc.tensor.matmul_mx(
                out=dw_bank[i][:],
                lhsT=x_codes[g][:, cols].bitcast(E4M3X4), lhsT_scale=x_scales[g][:, cols],
                rhs=dv_codes[g][:].bitcast(E5M2X4), rhs_scale=dv_scales[g][:],
                start=(g == 0), stop=(g == GROUPS - 1),
            )

        def finish_dw(i, copy):
            copy(
                out=dw[i][:].rearrange("p (b q r) -> p b q r", q=4, r=8),
                in_=dw_bank[i][:].rearrange("p (q b r) -> p b q r", q=4, r=8),
            )
            nc.sync.dma_start(out=out_1[i * P : (i + 1) * P, :], in_=dw[i][:])

        VC = nc.vector.tensor_copy
        SC = nc.scalar.copy

        def sort_w(c, u, copy):
            copy(
                out=w_sorted[:].rearrange("p (c u b r e) -> p c u b r e", c=4, u=2, r=8, e=2)[:, c, u],
                in_=w_raw[:].rearrange("p (c b u e r) -> p c u b r e", c=4, u=2, e=2, r=8)[:, c, u],
            )

        w_words = w_sorted[:].bitcast(F32)
        w_bank = {}

        def transpose_w(k):
            w_bank[k] = bank("dx_bank", (P, 2, 2, P))
            for c in range(2):
                for u in range(2):
                    at = (4 * k + 2 * c + u) * P
                    nc.tensor.transpose(w_bank[k][:, c, u, :], w_words[:, at : at + P], ident[:])

        def copy_w(k, copy):
            copy(
                out=w_t[:].bitcast(F32).rearrange("k (p c u) -> k p c u", c=4, u=2)[:, :, 2 * k : 2 * k + 2, :],
                in_=w_bank[k][:].rearrange("k c u p -> k p c u"),
            )

        def quantize_w():
            nc.vector.quantize_mx(out=w_codes[:].bitcast(E4M3X4), scales=w_scales[:], in_=w_t[:])

        def sigmoid_gate(h):
            nc.scalar.activation(out=sig_g[:, HALF[h]], in_=zg[:, HALF[h]], func=SIGMOID)

        def sigmoid_scale(h):
            nc.scalar.activation(out=sig_s[:, HALF[h]], in_=zs[:, HALF[h]], func=SIGMOID, scale=2.0)

        def make_m(h):
            nc.vector.scalar_tensor_tensor(
                out=m[:, HALF[h]], in0=sig_g[:, HALF[h]], scalar=2.0, in1=sig_s[:, HALF[h]], op0=MULT, op1=MULT
            )

        def tick(tile):
            nc.tensor.matmul(tile, lhsT=idle[:], rhs=idle[:], start=True, stop=True)

        def tick_dv(g, h):
            dv_bank[g, h] = bank("dv_bank", (P, 4, P))
            tick(dv_bank[g, h][:, 0, :])

        def tick_dx(g, t):
            dx_bank[g, t // 2, t % 2] = bank("dx_bank")
            tick(dx_bank[g, t // 2, t % 2][:, :P])

        def transpose_half(g, h):
            words = dv[g][:].rearrange("p q n t -> p (q n t)").bitcast(F32)
            if (g, h) not in dv_bank:
                dv_bank[g, h] = bank("dv_bank", (P, 4, P))
            for q in range(4):
                nc.tensor.transpose(dv_bank[g, h][:, q, :], words[:, q * 256 + h : (q + 1) * 256 : 2], ident[:])

        def copy_dvt_by(g, h, copy):
            copy(
                out=dvt[g, h][:].rearrange("k (e p q) -> k e p q", e=2, q=4),
                in_=dv_bank[g, h][:].bitcast(BF16).rearrange("k q (p e) -> k e p q", e=2),
            )

        def mx_dx(g, t):
            h, e = t // 2, t % 2
            if (g, h, e) not in dx_bank:
                dx_bank[g, h, e] = bank("dx_bank")
            cols = slice(e * P, (e + 1) * P)
            nc.tensor.matmul_mx(
                out=dx_bank[g, h, e][:],
                lhsT=dvt_codes[g, h][:, cols].bitcast(E5M2X4), lhsT_scale=dvt_scales[g, h][:, cols],
                rhs=w_codes[:].bitcast(E4M3X4), rhs_scale=w_scales[:],
                start=True, stop=True,
            )

        def store_row(g, t):
            nc.sync.dma_start(out=dx_hbm[g][:, t, :], in_=dx[g, t // 2][:, t % 2, :])

        def x_half(g, j, copy):
            copy(
                out=xg[g][:].rearrange("p (j c i t) -> p j c t i", j=2, i=4, t=4)[:, j],
                in_=x_raw[g][:].rearrange("p (t j c i) -> p j c t i", t=4, j=2, i=4)[:, j],
            )

        def x_quarter(g, k):
            nc.gpsimd.tensor_scalar(
                out=xg[g][:].rearrange("p (k n t) -> p k n t", k=4, t=4)[:, k],
                in0=x_raw[g][:].rearrange("p (t k n) -> p k n t", t=4, k=4)[:, k],
                scalar1=1.0, scalar2=0.0, op0=MULT, op1=ADD,
            )

        def copy_dw(i, copy):
            copy(
                out=dw[i][:].rearrange("p (b q r) -> p b q r", q=4, r=8),
                in_=dw_bank[i][:].rearrange("p (q b r) -> p b q r", q=4, r=8),
            )

        def store_dw(i):
            nc.sync.dma_start(out=out_1[i * P : (i + 1) * P, :], in_=dw[i][:])

        warm_bank = bank("dw_bank")
        tick(warm_bank[:, :P])
        tick(warm_bank[:, :P])
        tick(warm_bank[:, :P])
        tick(warm_bank[:, :P])
        sigmoid_gate(0)
        tick(warm_bank[:, :P])
        sigmoid_scale(0)
        sigmoid_scale(1)
        make_m(0)
        sigmoid_gate(1)
        spread_m(0, HALF[0])
        make_m(1)
        spread_m(0, HALF[1])
        spread_m(1)
        sort_w(3, 0, SC)
        multiply(0, 0)
        sort_w(2, 1, SC)
        sort_w(3, 1, SC)
        multiply(0, 1)
        sort_w(2, 0, SC)
        x_quarter(0, 2)
        multiply(0, 2)
        sort_w(0, 1, SC)
        transpose_w(1)
        sort_w(1, 1, SC)
        x_quarter(0, 1)
        multiply(0, 3)
        spread_m(2)
        sort_w(0, 0, SC)
        sort_w(1, 0, SC)
        multiply(1, 0)
        copy_w(1, SC)
        multiply(1, 1)
        transpose_w(0)
        x_quarter(1, 0)
        transpose_half(0, 1)
        multiply(1, 2)
        copy_w(0, SC)
        transpose_half(0, 0)
        x_quarter(1, 3)
        multiply(1, 3)
        copy_dvt_by(0, 1, SC)
        spread_m(3)
        x_quarter(1, 2)
        multiply(2, 0)
        x_quarter(0, 3)
        copy_dvt_by(0, 0, SC)
        multiply(2, 1)
        transpose_half(1, 0)
        x_quarter(2, 0)
        multiply(2, 2)
        tick_dx(0, 1)
        copy_dvt_by(1, 0, SC)
        transpose_half(1, 1)
        quantize_w()
        tick_dx(0, 0)
        quantize_dvt(0, 0)
        multiply(2, 3)
        x_quarter(2, 3)
        copy_dvt_by(1, 1, SC)
        mx_dx(0, 1)
        multiply(3, 0)
        tick_dv(2, 0)
        x_quarter(1, 1)
        mx_dx(0, 0)
        copy_dx(0, 0, 1, SC)
        transpose_half(2, 0)
        quantize_dvt(0, 1)
        quantize_dvt(1, 1)
        copy_dx(0, 0, 0, SC)
        tick_dx(1, 2)
        multiply(3, 1)
        x_quarter(2, 2)
        tick_dx(1, 3)
        copy_dvt_by(2, 0, SC)
        mx_dx(1, 2)
        multiply(3, 2)
        x_quarter(0, 0)
        mx_dx(1, 3)
        mx_dx(0, 3)
        multiply(3, 3)
        transpose_half(2, 1)
        x_quarter(2, 1)
        copy_dx(1, 1, 0, SC)
        copy_dx(1, 1, 1, VC)
        copy_dx(0, 1, 1, SC)
        tick_dx(0, 2)
        mx_dx(0, 2)
        quantize_dvt(1, 0)
        copy_dvt_by(2, 1, SC)
        store_dx(1, 1)
        quantize_dv(1)
        mx_dx(1, 1)
        transpose_half(3, 0)
        quantize_x(0)
        copy_dx(0, 1, 0, SC)
        tick_dv(3, 1)
        quantize_dvt(2, 0)
        transpose_half(3, 1)
        copy_dvt_by(3, 0, SC)
        quantize_x(1)
        store_dx(0, 1)
        mx_dx(2, 0)
        store_dx(0, 0)
        quantize_dvt(2, 1)
        mx_dx(1, 0)
        quantize_dv(0)
        copy_dx(1, 0, 1, SC)
        x_half(3, 1, VC)
        copy_dx(2, 0, 0, SC)
        mx_dx(2, 2)
        multiply_dw(0, 0, "dw_bank")
        copy_dx(1, 0, 0, SC)
        quantize_x(2)
        mx_dx(2, 1)
        multiply_dw(3, 0, "dv_bank")
        copy_dvt_by(3, 1, SC)
        quantize_dvt(3, 0)
        multiply_dw(0, 1, "dw_bank")
        store_dx(1, 0)
        multiply_dw(2, 0, "m_rep")
        copy_dx(2, 0, 1, VC)
        mx_dx(2, 3)
        multiply_dw(1, 0, "m_rep")
        quantize_dv(2)
        copy_dx(2, 1, 0, SC)
        mx_dx(3, 0)
        store_dx(2, 0)
        multiply_dw(3, 1, "dv_bank")
        quantize_dvt(3, 1)
        copy_dx(2, 1, 1, SC)
        mx_dx(3, 1)
        x_half(3, 0, VC)
        multiply_dw(2, 1, "m_rep")
        copy_dx(3, 0, 0, SC)
        multiply_dw(2, 2, "m_rep")
        store_dx(2, 1)
        mx_dx(3, 2)
        quantize_dv(3)
        copy_dx(3, 0, 1, SC)
        mx_dx(3, 3)
        multiply_dw(0, 2, "dw_bank")
        quantize_x(3)
        copy_dx(3, 1, 0, SC)
        store_dx(3, 0)
        copy_dx(3, 1, 1, VC)
        multiply_dw(2, 3, "m_rep")
        multiply_dw(0, 3, "dw_bank")
        multiply_dw(1, 1, "m_rep")
        copy_dw(2, VC)
        store_dx(3, 1)
        multiply_dw(3, 2, "dv_bank")
        multiply_dw(3, 3, "dv_bank")
        copy_dw(0, VC)
        multiply_dw(1, 2, "m_rep")
        store_dw(2)
        multiply_dw(1, 3, "m_rep")
        copy_dw(3, VC)
        store_dw(0)
        copy_dw(1, VC)
        store_dw(3)
        store_dw(1)
